import numpy as np
import ml_dtypes


def mxq(x, axis, fmt="e4m3"):
    dtype, down = {"e4m3": (ml_dtypes.float8_e4m3fn, 7), "e5m2": (ml_dtypes.float8_e5m2, 14)}[fmt]
    v = np.moveaxis(np.asarray(x, np.float32).astype(ml_dtypes.bfloat16).astype(np.float64), axis, -1)
    blocks = v.reshape(v.shape[:-1] + (-1, 32))
    amax = np.abs(blocks).max(-1, keepdims=True)
    byte = np.maximum(np.where(amax > 0, np.frexp(amax)[1] - 1 + 127, 0) - down, 1)
    scale = np.exp2(byte - 127.0)
    codes = (blocks / scale).astype(np.float32).astype(dtype).astype(np.float64)
    return np.moveaxis((codes * scale).reshape(v.shape), -1, axis)


WIDE = False


def mx_kscale(k):
    if not WIDE:
        return np.ones(k)
    levels = np.array([10, -10, 5, -5, 0])
    if k % 512:
        return np.exp2(np.random.permutation(np.resize(levels, k // 32))).repeat(32)
    a = np.empty((k // 512, 16))
    for p in range(k // 512):
        a[p, :8] = np.random.permutation(np.resize(levels, 8))
        for g in range(8):
            far = levels[np.abs(levels - a[p, g]) >= 10]
            a[p, g + 8] = far[np.random.randint(len(far))]
    return np.exp2(a.ravel()).repeat(32)


BF16 = ml_dtypes.bfloat16


def bf(x):
    return np.asarray(x, np.float32).astype(BF16)


def f64(x):
    return np.asarray(x).astype(np.float64)


B, L, C, D, H, Q = 8, 1024, 512, 256, 8, 256
EPS = 1e-5


def layer_norm(v, w, b):
    mu = v.mean(-1, keepdims=True)
    var = v.var(-1, keepdims=True)
    return (v - mu) * (1.0 / np.sqrt(var + EPS)) * w + b


def setup_inputs():
    s = mx_kscale(C)
    mag = 10.0 ** (-2.5 * np.random.uniform(size=(B, L, 1)))
    x = (np.random.standard_normal((B, L, C)) + 0.5 * np.random.standard_normal((B, L, 1))) * mag
    return {"x": bf(x),
            "ln_k_w": bf((1.0 + 0.1 * np.random.standard_normal(C)) * s),
            "ln_k_b": bf(0.1 * np.random.standard_normal(C) * s),
            "Wk": bf(np.random.standard_normal((D, C)) / np.sqrt(C) / s[None, :]),
            "Wv": bf(np.random.standard_normal((D, C)) / np.sqrt(C) / s[None, :]),
            "bk": bf(0.1 * np.random.standard_normal(D)),
            "bv": bf(0.1 * np.random.standard_normal(D))}


def reference(x, ln_k_w, ln_k_b, Wk, Wv, bk, bv):
    xk = mxq(layer_norm(f64(x), f64(ln_k_w), f64(ln_k_b)), 2, "e4m3")
    k = (xk @ mxq(f64(Wk).T, 0, "e4m3")) + f64(bk)
    v = (xk @ mxq(f64(Wv).T, 0, "e4m3")) + f64(bv)
    return k, v

@@ -1,0 +1,277 @@
+from contextlib import ExitStack
+
+import concourse.mybir as mybir
+from concourse.masks import make_identity
+
+FP32 = mybir.dt.float32
+BF16 = mybir.dt.bfloat16
+U32 = mybir.dt.uint32
+U8 = mybir.dt.uint8
+FP8X4 = mybir.dt.float8_e4m3fn_x4
+ALU = mybir.AluOpType
+ACT = mybir.ActivationFunctionType
+
+P = 128
+PACK = 4
+FEATS = 512
+TOKENS = 8192
+HALF = 256
+OUTS = 2 * HALF
+NT = 4
+GROUP = NT * P
+NG = TOKENS // GROUP
+EPS = 1e-5
+LC = 2
+LE = 3
+LQ = 4
+
+FLOPS = 2 * TOKENS * FEATS * OUTS
+
+
+def sg_bank(g, n):
+    return n == 3 and g % 2 == 0
+
+
+def t4_on_vector(g):
+    return False
+
+
+def tile_attentionalpoolerwmasking_pa_t_kernel(tc, x, ln_k_w, ln_k_b, Wk, Wv, bk, bv, out_0, out_1):
+    nc = tc.nc
+    xf = x.flatten_outer_dims()
+    kf = out_0.flatten_outer_dims()
+    vf = out_1.flatten_outer_dims()
+
+    with ExitStack() as ctx:
+        ctx.enter_context(tc.manual_schedule())
+        const = ctx.enter_context(tc.tile_pool(name="const", bufs=1))
+        xin = ctx.enter_context(tc.tile_pool(name="xin", bufs=NG))
+        small = ctx.enter_context(tc.tile_pool(name="small", bufs=6))
+        xh = ctx.enter_context(tc.tile_pool(name="xh", bufs=2))
+        pl = ctx.enter_context(tc.tile_pool(name="pl", bufs=2))
+        gr = ctx.enter_context(tc.tile_pool(name="gr", bufs=3))
+        cd = ctx.enter_context(tc.tile_pool(name="cd", bufs=2))
+        rs = ctx.enter_context(tc.tile_pool(name="rs", bufs=4))
+        psum = ctx.enter_context(tc.psum_pool(name="psum", bufs=4))
+
+        st = {}
+
+        def load(g):
+            x_sb = xin.tile([P, NT, FEATS], BF16, tag="x", name="x_sb%d" % g)
+            st[("x", g)] = x_sb
+            nc.sync.dma_start(
+                out=x_sb[:], in_=xf[g * GROUP : (g + 1) * GROUP, :].rearrange("(p n) f -> p n f", n=NT)
+            )
+
+        def stats_open(g):
+            st[("bn", g)] = small.tile([P, NT, 6], FP32, tag="bn", name="bn%d" % g)
+
+        def stats_tile(g, n):
+            nc.vector.bn_stats(out=st[("bn", g)][:, n, :], in_=st[("x", g)][:, n, :])
+
+        def stats_close(g):
+            mv = small.tile([P, NT, 2], FP32, tag="mv", name="mv%d" % g)
+            for n in range(NT):
+                nc.vector.bn_aggr(out=mv[:, n, :], in_=st[("bn", g)][:, n, :])
+            st[("mv", g)] = mv
+
+        def neg_mean(g):
+            negm = small.tile([P, NT], FP32, tag="negm", name="negm%d" % g)
+            nc.gpsimd.tensor_scalar(
+                out=negm[:], in0=st[("mv", g)][:, :, 0], scalar1=-1.0, scalar2=0.0, op0=ALU.mult, op1=ALU.add
+            )
+            st[("negm", g)] = negm
+
+        def root(g):
+            std = small.tile([P, NT], FP32, tag="std", name="std%d" % g)
+            nc.scalar.activation(out=std[:], in_=st[("mv", g)][:, :, 1], func=ACT.Sqrt, bias=EPS, scale=1.0)
+            st[("std", g)] = std
+
+        def recip(g):
+            rstd = small.tile([P, NT], FP32, tag="rstd", name="rstd%d" % g)
+            nc.vector.reciprocal(out=rstd[:], in_=st[("std", g)][:])
+            st[("rstd", g)] = rstd
+
+        def normalise(g):
+            xhat = xh.tile([P, NT, FEATS], FP32, tag="xhat", name="xhat%d" % g)
+            for n in range(NT):
+                nc.gpsimd.tensor_scalar(
+                    out=xhat[:, n, :].rearrange("p (t q) -> p t q", t=PACK),
+                    in0=st[("x", g)][:, n, :].rearrange("p (q t) -> p t q", t=PACK),
+                    scalar1=st[("negm", g)][:, n : n + 1],
+                    scalar2=st[("rstd", g)][:, n : n + 1],
+                    op0=ALU.add,
+                    op1=ALU.mult,
+                )
+            st[("xhat", g)] = xhat
+
+        def transposes(g):
+            xhat = st[("xhat", g)]
+            banks = []
+            for j in range(PACK):
+                tb = psum.tile([P, GROUP], FP32, tag="t", name="tb%d_%d" % (g, j))
+                banks.append(tb)
+            for j in range(PACK):
+                for n in range(NT):
+                    nc.tensor.transpose(
+                        banks[j][:, n * P : (n + 1) * P], xhat[:, n, j * P : (j + 1) * P], ident_f[:]
+                    )
+            st[("banks", g)] = banks
+
+        def affine(g):
+            planes = pl.tile([P, PACK, GROUP], BF16, tag="planes", name="planes%d" % g)
+            for j in range(PACK):
+                nc.scalar.activation(
+                    out=planes[:, j, :],
+                    in_=st[("banks", g)][j][:],
+                    func=ACT.Identity,
+                    scale=ln_col[:, j : j + 1],
+                    bias=ln_col[:, PACK + j : PACK + j + 1],
+                )
+            st[("planes", g)] = planes
+
+        def regroup(g):
+            grouped = gr.tile([P, GROUP, PACK], BF16, tag="grouped", name="grouped%d" % g, align_bytes=64)
+            dst = grouped[:].rearrange("p (c i) t -> p c t i", i=4)
+            src = st[("planes", g)][:].rearrange("p t (c i) -> p c t i", i=4)
+            if t4_on_vector(g):
+                nc.vector.tensor_copy(out=dst, in_=src)
+            else:
+                nc.scalar.copy(out=dst, in_=src)
+            st[("grouped", g)] = grouped
+
+        def quantise(g):
+            codes = cd.tile([P, GROUP], U32, tag="codes", name="codes%d" % g, align_bytes=64)
+            scl = cd.tile([P, GROUP], U8, tag="scl", name="scl%d" % g, align_bytes=64)
+            nc.vector.quantize_mx(
+                out=codes[:].bitcast(FP8X4),
+                scales=scl[:],
+                in_=st[("grouped", g)][:].rearrange("p c t -> p (c t)"),
+            )
+            st[("codes", g)] = codes
+            st[("scl", g)] = scl
+
+        def project(g):
+            obs = []
+            for n in range(NT):
+                ob = psum.tile([P, OUTS], FP32, tag="o", name="ob%d_%d" % (g, n))
+                nc.tensor.matmul_mx(
+                    out=ob[:],
+                    lhsT=st[("codes", g)][:, n * P : (n + 1) * P].bitcast(FP8X4),
+                    lhsT_scale=st[("scl", g)][:, n * P : (n + 1) * P],
+                    rhs=w_codes[:].bitcast(FP8X4),
+                    rhs_scale=w_scales[:],
+                    start=True,
+                    stop=True,
+                )
+                obs.append(ob)
+            st[("obs", g)] = obs
+
+        def finish(g):
+            res = rs.tile([P, 2, NT, HALF], FP32, tag="res", name="res%d" % g)
+            bias_v = bias_sb[:].rearrange("p (h o) -> p h o", h=2)
+            for n in range(NT):
+                ob_v = st[("obs", g)][n][:].rearrange("p (h o) -> p h o", h=2)
+                if sg_bank(g, n):
+                    nc.scalar.copy(out=res[:, :, n, :], in_=ob_v)
+                    nc.gpsimd.tensor_tensor(out=res[:, :, n, :], in0=res[:, :, n, :], in1=bias_v, op=ALU.add)
+                else:
+                    nc.vector.tensor_tensor(out=res[:, :, n, :], in0=ob_v, in1=bias_v, op=ALU.add)
+            rows = slice(g * GROUP, (g + 1) * GROUP)
+            nc.sync.dma_start(out=kf[rows, :].rearrange("(p n) o -> p n o", n=NT), in_=res[:, 0, :, :])
+            nc.sync.dma_start(out=vf[rows, :].rearrange("(p n) o -> p n o", n=NT), in_=res[:, 1, :, :])
+
+        def stats(g):
+            stats_open(g)
+            for n in range(NT):
+                stats_tile(g, n)
+            stats_close(g)
+
+        def scalars_and_normalise(g):
+            recip(g)
+            neg_mean(g)
+            normalise(g)
+
+        def live(g):
+            return 0 <= g < NG
+
+        x_first = xin.tile([P, NT, FEATS], BF16, tag="x", name="x_sb0")
+        st[("x", 0)] = x_first
+        for n in range(NT):
+            nc.sync.dma_start(
+                out=x_first[:, n, :], in_=xf[0:GROUP, :].rearrange("(p n) f -> p n f", n=NT)[:, n, :]
+            )
+        w_raw = const.tile([P, 4, FEATS], BF16)
+        nc.scalar.dma_start(out=w_raw[:, 0:2, :], in_=Wk.rearrange("(c p) f -> p c f", p=P))
+        nc.scalar.dma_start(out=w_raw[:, 2:4, :], in_=Wv.rearrange("(c p) f -> p c f", p=P))
+        ln_w_raw = const.tile([P, PACK], BF16)
+        ln_b_raw = const.tile([P, PACK], BF16)
+        nc.scalar.dma_start(out=ln_w_raw[:], in_=ln_k_w.rearrange("(p t) -> p t", t=PACK))
+        nc.scalar.dma_start(out=ln_b_raw[:], in_=ln_k_b.rearrange("(p t) -> p t", t=PACK))
+        for g in range(1, NG):
+            load(g)
+        ident_b = const.tile([P, P], BF16)
+        make_identity(nc, ident_b[:])
+        ident_f = const.tile([P, P], FP32)
+        make_identity(nc, ident_f[:])
+
+        stats(0)
+        root(0)
+        stats_open(1)
+        stats_tile(1, 0)
+        scalars_and_normalise(0)
+
+        ln_col = const.tile([P, 8], FP32)
+        nc.scalar.copy(out=ln_col[:, 0:PACK], in_=ln_w_raw[:])
+        nc.scalar.copy(out=ln_col[:, PACK : 2 * PACK], in_=ln_b_raw[:])
+
+        w_grp = const.tile([P, OUTS, PACK], BF16, align_bytes=64)
+        for h in range(2):
+            wt = psum.tile([P, PACK, HALF], BF16, tag="t", name="wt%d" % h)
+            for j in range(PACK):
+                for c in range(2):
+                    nc.tensor.transpose(
+                        wt[:, j, c * P : (c + 1) * P], w_raw[:, 2 * h + c, j:FEATS:PACK], ident_b[:]
+                    )
+            nc.scalar.copy(out=w_grp[:, h * HALF : (h + 1) * HALF, :], in_=wt[:].rearrange("p j o -> p o j"))
+        w_codes = const.tile([P, OUTS], U32, align_bytes=64)
+        w_scales = const.tile([P, OUTS], U8, align_bytes=64)
+        bias_sb = const.tile([P, OUTS], BF16)
+
+        transposes(0)
+        for n in range(1, NT):
+            stats_tile(1, n)
+        stats_close(1)
+        root(1)
+        stats_open(2)
+        stats_tile(2, 0)
+        scalars_and_normalise(1)
+        nc.scalar.dma_start(out=bias_sb[:, 0:HALF], in_=bk.partition_broadcast(P))
+        nc.scalar.dma_start(out=bias_sb[:, HALF:OUTS], in_=bv.partition_broadcast(P))
+        for n in range(1, NT):
+            stats_tile(2, n)
+        stats_close(2)
+
+        for i in range(NG + 2):
+            if live(i):
+                affine(i)
+            if live(i + 1):
+                transposes(i + 1)
+            if live(i + 2):
+                root(i + 2)
+            if live(i):
+                regroup(i)
+            if live(i + 3):
+                stats(i + 3)
+            if live(i + 2):
+                scalars_and_normalise(i + 2)
+            if i == 0:
+                nc.vector.quantize_mx(
+                    out=w_codes[:].bitcast(FP8X4), scales=w_scales[:], in_=w_grp[:].rearrange("p o j -> p (o j)")
+                )
+            if live(i - 1):
+                quantise(i - 1)
+            if live(i - 2):
+                finish(i - 2)
+            if live(i - 1):
+                project(i - 1)

@@ -21,15 +21,13 @@ NT = 4
 GROUP = NT * P
 NG = TOKENS // GROUP
 EPS = 1e-5
-LC = 2
-LE = 3
-LQ = 4
+SOON = NG - 3
 
 FLOPS = 2 * TOKENS * FEATS * OUTS
 
 
 def sg_bank(g, n):
-    return n == 3 and g % 2 == 0
+    return n == 3 and g % 2 == 0 and g < SOON
 
 
 def t4_on_vector(g):
@@ -111,12 +109,48 @@ def tile_attentionalpoolerwmasking_pa_t_kernel(tc, x, ln_k_w, ln_k_b, Wk, Wv, bk
             for j in range(PACK):
                 tb = psum.tile([P, GROUP], FP32, tag="t", name="tb%d_%d" % (g, j))
                 banks.append(tb)
-            for j in range(PACK):
-                for n in range(NT):
-                    nc.tensor.transpose(
-                        banks[j][:, n * P : (n + 1) * P], xhat[:, n, j * P : (j + 1) * P], ident_f[:]
-                    )
+            if g == 0:
+                order = [(j, n) for n in range(NT) for j in range(PACK)]
+            else:
+                order = [(j, n) for j in range(PACK) for n in range(NT)]
+            for j, n in order:
+                nc.tensor.transpose(banks[j][:, n * P : (n + 1) * P], xhat[:, n, j * P : (j + 1) * P], ident_f[:])
             st[("banks", g)] = banks
+
+        def first_group():
+            stats_open(0)
+            mv = small.tile([P, NT, 2], FP32, tag="mv", name="mv0")
+            std = small.tile([P, NT], FP32, tag="std", name="std0")
+            negm = small.tile([P, NT], FP32, tag="negm", name="negm0")
+            rstd = small.tile([P, NT], FP32, tag="rstd", name="rstd0")
+            xhat = xh.tile([P, NT, FEATS], FP32, tag="xhat", name="xhat0")
+            st[("xhat", 0)] = xhat
+            stats_open(1)
+            for lo in (0, 2):
+                hi = lo + 2
+                if lo == 0:
+                    stats_tile(0, 0)
+                    stats_tile(0, 1)
+                else:
+                    stats_tile(0, 3)
+                for n in range(lo, hi):
+                    nc.vector.bn_aggr(out=mv[:, n, :], in_=st[("bn", 0)][:, n, :])
+                nc.scalar.activation(out=std[:, lo:hi], in_=mv[:, lo:hi, 1], func=ACT.Sqrt, bias=EPS, scale=1.0)
+                nc.scalar.activation(out=negm[:, lo:hi], in_=mv[:, lo:hi, 0], func=ACT.Copy, scale=-1.0)
+                if lo == 0:
+                    stats_tile(0, 2)
+                else:
+                    stats_tile(1, 0)
+                nc.vector.reciprocal(out=rstd[:, lo:hi], in_=std[:, lo:hi])
+                for n in range(lo, hi):
+                    nc.gpsimd.tensor_scalar(
+                        out=xhat[:, n, :].rearrange("p (t q) -> p t q", t=PACK),
+                        in0=st[("x", 0)][:, n, :].rearrange("p (q t) -> p t q", t=PACK),
+                        scalar1=negm[:, n : n + 1],
+                        scalar2=rstd[:, n : n + 1],
+                        op0=ALU.add,
+                        op1=ALU.mult,
+                    )
 
         def affine(g):
             planes = pl.tile([P, PACK, GROUP], BF16, tag="planes", name="planes%d" % g)
@@ -181,6 +215,56 @@ def tile_attentionalpoolerwmasking_pa_t_kernel(tc, x, ln_k_w, ln_k_b, Wk, Wv, bk
             nc.sync.dma_start(out=kf[rows, :].rearrange("(p n) o -> p n o", n=NT), in_=res[:, 0, :, :])
             nc.sync.dma_start(out=vf[rows, :].rearrange("(p n) o -> p n o", n=NT), in_=res[:, 1, :, :])
 
+        def regroup_by_tile(g):
+            grouped = gr.tile([P, GROUP, PACK], BF16, tag="grouped", name="grouped%d" % g, align_bytes=64)
+            for n in range(NT):
+                cols = slice(n * P, (n + 1) * P)
+                nc.scalar.copy(
+                    out=grouped[:, cols, :].rearrange("p (c i) t -> p c t i", i=4),
+                    in_=st[("planes", g)][:, :, cols].rearrange("p t (c i) -> p c t i", i=4),
+                )
+            st[("grouped", g)] = grouped
+
+        def end_by_tile(g):
+            codes = cd.tile([P, GROUP], U32, tag="codes", name="codes%d" % g, align_bytes=64)
+            scl = cd.tile([P, GROUP], U8, tag="scl", name="scl%d" % g, align_bytes=64)
+            res = rs.tile([P, 2, NT, HALF], FP32, tag="res", name="res%d" % g)
+            bias_v = bias_sb[:].rearrange("p (h o) -> p h o", h=2)
+            rows = slice(g * GROUP, (g + 1) * GROUP)
+            obs = []
+
+            def front(n):
+                cols = slice(n * P, (n + 1) * P)
+                nc.vector.quantize_mx(
+                    out=codes[:, cols].bitcast(FP8X4),
+                    scales=scl[:, cols],
+                    in_=st[("grouped", g)][:, cols, :].rearrange("p c t -> p (c t)"),
+                )
+                ob = psum.tile([P, OUTS], FP32, tag="o", name="ob%d_%d" % (g, n))
+                nc.tensor.matmul_mx(
+                    out=ob[:],
+                    lhsT=codes[:, cols].bitcast(FP8X4),
+                    lhsT_scale=scl[:, cols],
+                    rhs=w_codes[:].bitcast(FP8X4),
+                    rhs_scale=w_scales[:],
+                    start=True,
+                    stop=True,
+                )
+                obs.append(ob)
+
+            def back(n):
+                nc.vector.tensor_tensor(
+                    out=res[:, :, n, :], in0=obs[n][:].rearrange("p (h o) -> p h o", h=2), in1=bias_v, op=ALU.add
+                )
+                nc.sync.dma_start(out=kf[rows, :].rearrange("(p n) o -> p n o", n=NT)[:, n, :], in_=res[:, 0, n, :])
+                nc.sync.dma_start(out=vf[rows, :].rearrange("(p n) o -> p n o", n=NT)[:, n, :], in_=res[:, 1, n, :])
+
+            front(0)
+            for n in range(1, NT):
+                front(n)
+                back(n - 1)
+            back(NT - 1)
+
         def stats(g):
             stats_open(g)
             for n in range(NT):
@@ -215,11 +299,7 @@ def tile_attentionalpoolerwmasking_pa_t_kernel(tc, x, ln_k_w, ln_k_b, Wk, Wv, bk
         ident_f = const.tile([P, P], FP32)
         make_identity(nc, ident_f[:])
 
-        stats(0)
-        root(0)
-        stats_open(1)
-        stats_tile(1, 0)
-        scalars_and_normalise(0)
+        first_group()
 
         ln_col = const.tile([P, 8], FP32)
         nc.scalar.copy(out=ln_col[:, 0:PACK], in_=ln_w_raw[:])
@@ -227,7 +307,7 @@ def tile_attentionalpoolerwmasking_pa_t_kernel(tc, x, ln_k_w, ln_k_b, Wk, Wv, bk
 
         w_grp = const.tile([P, OUTS, PACK], BF16, align_bytes=64)
         for h in range(2):
-            wt = psum.tile([P, PACK, HALF], BF16, tag="t", name="wt%d" % h)
+            wt = psum.tile([P, PACK, HALF], BF16, tag="o", name="wt%d" % h)
             for j in range(PACK):
                 for c in range(2):
                     nc.tensor.transpose(
@@ -252,14 +332,22 @@ def tile_attentionalpoolerwmasking_pa_t_kernel(tc, x, ln_k_w, ln_k_b, Wk, Wv, bk
             stats_tile(2, n)
         stats_close(2)
 
-        for i in range(NG + 2):
+        for i in range(NG + 1):
+            late = SOON < i < NG
+            if i == NG - 1:
+                end_by_tile(i - 1)
+            elif late:
+                quantise(i - 1)
+                project(i - 1)
             if live(i):
                 affine(i)
             if live(i + 1):
                 transposes(i + 1)
             if live(i + 2):
                 root(i + 2)
-            if live(i):
+            if i >= NG - 2 and live(i):
+                regroup_by_tile(i)
+            elif live(i):
                 regroup(i)
             if live(i + 3):
                 stats(i + 3)
@@ -269,9 +357,16 @@ def tile_attentionalpoolerwmasking_pa_t_kernel(tc, x, ln_k_w, ln_k_b, Wk, Wv, bk
                 nc.vector.quantize_mx(
                     out=w_codes[:].bitcast(FP8X4), scales=w_scales[:], in_=w_grp[:].rearrange("p o j -> p (o j)")
                 )
-            if live(i - 1):
-                quantise(i - 1)
-            if live(i - 2):
-                finish(i - 2)
-            if live(i - 1):
-                project(i - 1)
+            if late and i < NG - 1:
+                finish(i - 1)
+            elif i == NG:
+                end_by_tile(NG - 1)
+            elif i <= SOON:
+                if live(i - 1):
+                    quantise(i - 1)
+                if live(i - 2):
+                    finish(i - 2)
+                if live(i - 1):
+                    project(i - 1)
+                if i == SOON:
+                    finish(i - 1)

@@ -27,11 +27,15 @@ FLOPS = 2 * TOKENS * FEATS * OUTS
 
 
 def sg_bank(g, n):
-    return n == 3 and g % 2 == 0 and g < SOON
+    return n == 3 and g % 2 == 0 and g < SOON - 1
 
 
 def t4_on_vector(g):
     return False
+
+
+def vector_tiles(g):
+    return NT - 1 if g == 1 else NT
 
 
 def tile_attentionalpoolerwmasking_pa_t_kernel(tc, x, ln_k_w, ln_k_b, Wk, Wv, bk, bv, out_0, out_1):
@@ -69,21 +73,46 @@ def tile_attentionalpoolerwmasking_pa_t_kernel(tc, x, ln_k_w, ln_k_b, Wk, Wv, bk
 
         def stats_close(g):
             mv = small.tile([P, NT, 2], FP32, tag="mv", name="mv%d" % g)
-            for n in range(NT):
+            for n in range(vector_tiles(g)):
                 nc.vector.bn_aggr(out=mv[:, n, :], in_=st[("bn", g)][:, n, :])
             st[("mv", g)] = mv
+            st[("negm", g)] = small.tile([P, NT], FP32, tag="negm", name="negm%d" % g)
+            st[("std", g)] = small.tile([P, NT], FP32, tag="std", name="std%d" % g)
 
         def neg_mean(g):
-            negm = small.tile([P, NT], FP32, tag="negm", name="negm%d" % g)
+            nv = vector_tiles(g)
             nc.gpsimd.tensor_scalar(
-                out=negm[:], in0=st[("mv", g)][:, :, 0], scalar1=-1.0, scalar2=0.0, op0=ALU.mult, op1=ALU.add
+                out=st[("negm", g)][:, 0:nv],
+                in0=st[("mv", g)][:, 0:nv, 0],
+                scalar1=-1.0,
+                scalar2=0.0,
+                op0=ALU.mult,
+                op1=ALU.add,
             )
-            st[("negm", g)] = negm
 
         def root(g):
-            std = small.tile([P, NT], FP32, tag="std", name="std%d" % g)
-            nc.scalar.activation(out=std[:], in_=st[("mv", g)][:, :, 1], func=ACT.Sqrt, bias=EPS, scale=1.0)
-            st[("std", g)] = std
+            nv = vector_tiles(g)
+            nc.scalar.activation(
+                out=st[("std", g)][:, 0:nv], in_=st[("mv", g)][:, 0:nv, 1], func=ACT.Sqrt, bias=EPS, scale=1.0
+            )
+
+        def scalar_stats(g):
+            for n in range(vector_tiles(g), NT):
+                one = slice(n, n + 1)
+                total = small.tile([P, 1], FP32, tag="total", name="total%d_%d" % (g, n))
+                spread = small.tile([P, 1], FP32, tag="spread", name="spread%d_%d" % (g, n))
+                junk = small.tile([P, FEATS], BF16, tag="junk", name="junk%d_%d" % (g, n))
+                nc.scalar.activation(out=junk[:], in_=st[("x", g)][:, n, :], func=ACT.Copy, accum_out=total[:])
+                nc.scalar.activation(out=st[("negm", g)][:, one], in_=total[:], func=ACT.Copy, scale=-1.0 / FEATS)
+                nc.scalar.activation(
+                    out=junk[:],
+                    in_=st[("x", g)][:, n, :],
+                    func=ACT.Square,
+                    bias=st[("negm", g)][:, one],
+                    scale=1.0,
+                    accum_out=spread[:],
+                )
+                nc.scalar.activation(out=st[("std", g)][:, one], in_=spread[:], func=ACT.Sqrt, bias=EPS, scale=1.0 / FEATS)
 
         def recip(g):
             rstd = small.tile([P, NT], FP32, tag="rstd", name="rstd%d" % g)
@@ -286,16 +315,14 @@ def tile_attentionalpoolerwmasking_pa_t_kernel(tc, x, ln_k_w, ln_k_b, Wk, Wv, bk
                 out=x_first[:, n, :], in_=xf[0:GROUP, :].rearrange("(p n) f -> p n f", n=NT)[:, n, :]
             )
         w_raw = const.tile([P, 4, FEATS], BF16)
-        nc.scalar.dma_start(out=w_raw[:, 0:2, :], in_=Wk.rearrange("(c p) f -> p c f", p=P))
-        nc.scalar.dma_start(out=w_raw[:, 2:4, :], in_=Wv.rearrange("(c p) f -> p c f", p=P))
+        nc.sync.dma_start(out=w_raw[:, 0:2, :], in_=Wk.rearrange("(c p) f -> p c f", p=P))
+        nc.sync.dma_start(out=w_raw[:, 2:4, :], in_=Wv.rearrange("(c p) f -> p c f", p=P))
         ln_w_raw = const.tile([P, PACK], BF16)
         ln_b_raw = const.tile([P, PACK], BF16)
         nc.scalar.dma_start(out=ln_w_raw[:], in_=ln_k_w.rearrange("(p t) -> p t", t=PACK))
         nc.scalar.dma_start(out=ln_b_raw[:], in_=ln_k_b.rearrange("(p t) -> p t", t=PACK))
         for g in range(1, NG):
             load(g)
-        ident_b = const.tile([P, P], BF16)
-        make_identity(nc, ident_b[:])
         ident_f = const.tile([P, P], FP32)
         make_identity(nc, ident_f[:])
 
@@ -306,22 +333,26 @@ def tile_attentionalpoolerwmasking_pa_t_kernel(tc, x, ln_k_w, ln_k_b, Wk, Wv, bk
         nc.scalar.copy(out=ln_col[:, PACK : 2 * PACK], in_=ln_b_raw[:])
 
         w_grp = const.tile([P, OUTS, PACK], BF16, align_bytes=64)
+        w_words = w_raw[:].bitcast(FP32)
         for h in range(2):
-            wt = psum.tile([P, PACK, HALF], BF16, tag="o", name="wt%d" % h)
-            for j in range(PACK):
+            wt = psum.tile([P, 2, HALF], FP32, tag="o", name="wt%d" % h)
+            for u in range(2):
                 for c in range(2):
                     nc.tensor.transpose(
-                        wt[:, j, c * P : (c + 1) * P], w_raw[:, 2 * h + c, j:FEATS:PACK], ident_b[:]
+                        wt[:, u, c * P : (c + 1) * P], w_words[:, 2 * h + c, u : FEATS // 2 : 2], ident_f[:]
                     )
-            nc.scalar.copy(out=w_grp[:, h * HALF : (h + 1) * HALF, :], in_=wt[:].rearrange("p j o -> p o j"))
+            nc.scalar.copy(
+                out=w_grp[:, h * HALF : (h + 1) * HALF, :].bitcast(FP32), in_=wt[:].rearrange("p u o -> p o u")
+            )
         w_codes = const.tile([P, OUTS], U32, align_bytes=64)
         w_scales = const.tile([P, OUTS], U8, align_bytes=64)
         bias_sb = const.tile([P, OUTS], BF16)
 
         transposes(0)
-        for n in range(1, NT):
+        for n in range(1, vector_tiles(1)):
             stats_tile(1, n)
         stats_close(1)
+        scalar_stats(1)
         root(1)
         stats_open(2)
         stats_tile(2, 0)
@@ -339,11 +370,13 @@ def tile_attentionalpoolerwmasking_pa_t_kernel(tc, x, ln_k_w, ln_k_b, Wk, Wv, bk
             elif late:
                 quantise(i - 1)
                 project(i - 1)
+            if live(i + 2) and i >= 2:
+                root(i + 2)
             if live(i):
                 affine(i)
             if live(i + 1):
                 transposes(i + 1)
-            if live(i + 2):
+            if live(i + 2) and i < 2:
                 root(i + 2)
             if i >= NG - 2 and live(i):
                 regroup_by_tile(i)

@@ -195,8 +195,8 @@ def tile_attentionalpoolerwmasking_pa_t_kernel(tc, x, ln_k_w, ln_k_b, Wk, Wv, bk
 
         def regroup(g):
             grouped = gr.tile([P, GROUP, PACK], BF16, tag="grouped", name="grouped%d" % g, align_bytes=64)
-            dst = grouped[:].rearrange("p (c i) t -> p c t i", i=4)
-            src = st[("planes", g)][:].rearrange("p t (c i) -> p c t i", i=4)
+            dst = grouped[:].rearrange("p (c i) t -> p c t i", i=8)
+            src = st[("planes", g)][:].rearrange("p t (c i) -> p c t i", i=8)
             if t4_on_vector(g):
                 nc.vector.tensor_copy(out=dst, in_=src)
             else:
@@ -249,8 +249,8 @@ def tile_attentionalpoolerwmasking_pa_t_kernel(tc, x, ln_k_w, ln_k_b, Wk, Wv, bk
             for n in range(NT):
                 cols = slice(n * P, (n + 1) * P)
                 nc.scalar.copy(
-                    out=grouped[:, cols, :].rearrange("p (c i) t -> p c t i", i=4),
-                    in_=st[("planes", g)][:, :, cols].rearrange("p t (c i) -> p c t i", i=4),
+                    out=grouped[:, cols, :].rearrange("p (c i) t -> p c t i", i=8),
+                    in_=st[("planes", g)][:, :, cols].rearrange("p t (c i) -> p c t i", i=8),
                 )
             st[("grouped", g)] = grouped
 

from contextlib import ExitStack

import concourse.mybir as mybir
from concourse.masks import make_identity

FP32 = mybir.dt.float32
BF16 = mybir.dt.bfloat16
U32 = mybir.dt.uint32
U8 = mybir.dt.uint8
FP8X4 = mybir.dt.float8_e4m3fn_x4
ALU = mybir.AluOpType
ACT = mybir.ActivationFunctionType

P = 128
PACK = 4
FEATS = 512
TOKENS = 8192
HALF = 256
OUTS = 2 * HALF
NT = 4
GROUP = NT * P
NG = TOKENS // GROUP
EPS = 1e-5
SOON = NG - 3

FLOPS = 2 * TOKENS * FEATS * OUTS


def sg_bank(g, n):
    return n == 3 and g % 2 == 0 and g < SOON - 1


def t4_on_vector(g):
    return False


def vector_tiles(g):
    return NT - 1 if g == 1 else NT


def tile_attentionalpoolerwmasking_pa_t_kernel(tc, x, ln_k_w, ln_k_b, Wk, Wv, bk, bv, out_0, out_1):
    nc = tc.nc
    xf = x.flatten_outer_dims()
    kf = out_0.flatten_outer_dims()
    vf = out_1.flatten_outer_dims()

    with ExitStack() as ctx:
        ctx.enter_context(tc.manual_schedule())
        const = ctx.enter_context(tc.tile_pool(name="const", bufs=1))
        xin = ctx.enter_context(tc.tile_pool(name="xin", bufs=NG))
        small = ctx.enter_context(tc.tile_pool(name="small", bufs=6))
        xh = ctx.enter_context(tc.tile_pool(name="xh", bufs=2))
        pl = ctx.enter_context(tc.tile_pool(name="pl", bufs=2))
        gr = ctx.enter_context(tc.tile_pool(name="gr", bufs=3))
        cd = ctx.enter_context(tc.tile_pool(name="cd", bufs=2))
        rs = ctx.enter_context(tc.tile_pool(name="rs", bufs=4))
        psum = ctx.enter_context(tc.psum_pool(name="psum", bufs=4))

        st = {}

        def load(g):
            x_sb = xin.tile([P, NT, FEATS], BF16, tag="x", name="x_sb%d" % g)
            st[("x", g)] = x_sb
            nc.sync.dma_start(
                out=x_sb[:], in_=xf[g * GROUP : (g + 1) * GROUP, :].rearrange("(p n) f -> p n f", n=NT)
            )

        def stats_open(g):
            st[("bn", g)] = small.tile([P, NT, 6], FP32, tag="bn", name="bn%d" % g)

        def stats_tile(g, n):
            nc.vector.bn_stats(out=st[("bn", g)][:, n, :], in_=st[("x", g)][:, n, :])

        def stats_close(g):
            mv = small.tile([P, NT, 2], FP32, tag="mv", name="mv%d" % g)
            for n in range(vector_tiles(g)):
                nc.vector.bn_aggr(out=mv[:, n, :], in_=st[("bn", g)][:, n, :])
            st[("mv", g)] = mv
            st[("negm", g)] = small.tile([P, NT], FP32, tag="negm", name="negm%d" % g)
            st[("std", g)] = small.tile([P, NT], FP32, tag="std", name="std%d" % g)

        def neg_mean(g):
            nv = vector_tiles(g)
            nc.gpsimd.tensor_scalar(
                out=st[("negm", g)][:, 0:nv],
                in0=st[("mv", g)][:, 0:nv, 0],
                scalar1=-1.0,
                scalar2=0.0,
                op0=ALU.mult,
                op1=ALU.add,
            )

        def root(g):
            nv = vector_tiles(g)
            nc.scalar.activation(
                out=st[("std", g)][:, 0:nv], in_=st[("mv", g)][:, 0:nv, 1], func=ACT.Sqrt, bias=EPS, scale=1.0
            )

        def scalar_stats(g):
            for n in range(vector_tiles(g), NT):
                one = slice(n, n + 1)
                total = small.tile([P, 1], FP32, tag="total", name="total%d_%d" % (g, n))
                spread = small.tile([P, 1], FP32, tag="spread", name="spread%d_%d" % (g, n))
                junk = small.tile([P, FEATS], BF16, tag="junk", name="junk%d_%d" % (g, n))
                nc.scalar.activation(out=junk[:], in_=st[("x", g)][:, n, :], func=ACT.Copy, accum_out=total[:])
                nc.scalar.activation(out=st[("negm", g)][:, one], in_=total[:], func=ACT.Copy, scale=-1.0 / FEATS)
                nc.scalar.activation(
                    out=junk[:],
                    in_=st[("x", g)][:, n, :],
                    func=ACT.Square,
                    bias=st[("negm", g)][:, one],
                    scale=1.0,
                    accum_out=spread[:],
                )
                nc.scalar.activation(out=st[("std", g)][:, one], in_=spread[:], func=ACT.Sqrt, bias=EPS, scale=1.0 / FEATS)

        def recip(g):
            rstd = small.tile([P, NT], FP32, tag="rstd", name="rstd%d" % g)
            nc.vector.reciprocal(out=rstd[:], in_=st[("std", g)][:])
            st[("rstd", g)] = rstd

        def normalise(g):
            xhat = xh.tile([P, NT, FEATS], FP32, tag="xhat", name="xhat%d" % g)
            for n in range(NT):
                nc.gpsimd.tensor_scalar(
                    out=xhat[:, n, :].rearrange("p (t q) -> p t q", t=PACK),
                    in0=st[("x", g)][:, n, :].rearrange("p (q t) -> p t q", t=PACK),
                    scalar1=st[("negm", g)][:, n : n + 1],
                    scalar2=st[("rstd", g)][:, n : n + 1],
                    op0=ALU.add,
                    op1=ALU.mult,
                )
            st[("xhat", g)] = xhat

        def transposes(g):
            xhat = st[("xhat", g)]
            banks = []
            for j in range(PACK):
                tb = psum.tile([P, GROUP], FP32, tag="t", name="tb%d_%d" % (g, j))
                banks.append(tb)
            if g == 0:
                order = [(j, n) for n in range(NT) for j in range(PACK)]
            else:
                order = [(j, n) for j in range(PACK) for n in range(NT)]
            for j, n in order:
                nc.tensor.transpose(banks[j][:, n * P : (n + 1) * P], xhat[:, n, j * P : (j + 1) * P], ident_f[:])
            st[("banks", g)] = banks

        def first_group():
            stats_open(0)
            mv = small.tile([P, NT, 2], FP32, tag="mv", name="mv0")
            std = small.tile([P, NT], FP32, tag="std", name="std0")
            negm = small.tile([P, NT], FP32, tag="negm", name="negm0")
            rstd = small.tile([P, NT], FP32, tag="rstd", name="rstd0")
            xhat = xh.tile([P, NT, FEATS], FP32, tag="xhat", name="xhat0")
            st[("xhat", 0)] = xhat
            stats_open(1)
            for lo in (0, 2):
                hi = lo + 2
                if lo == 0:
                    stats_tile(0, 0)
                    stats_tile(0, 1)
                else:
                    stats_tile(0, 3)
                for n in range(lo, hi):
                    nc.vector.bn_aggr(out=mv[:, n, :], in_=st[("bn", 0)][:, n, :])
                nc.scalar.activation(out=std[:, lo:hi], in_=mv[:, lo:hi, 1], func=ACT.Sqrt, bias=EPS, scale=1.0)
                nc.scalar.activation(out=negm[:, lo:hi], in_=mv[:, lo:hi, 0], func=ACT.Copy, scale=-1.0)
                if lo == 0:
                    stats_tile(0, 2)
                else:
                    stats_tile(1, 0)
                nc.vector.reciprocal(out=rstd[:, lo:hi], in_=std[:, lo:hi])
                for n in range(lo, hi):
                    nc.gpsimd.tensor_scalar(
                        out=xhat[:, n, :].rearrange("p (t q) -> p t q", t=PACK),
                        in0=st[("x", 0)][:, n, :].rearrange("p (q t) -> p t q", t=PACK),
                        scalar1=negm[:, n : n + 1],
                        scalar2=rstd[:, n : n + 1],
                        op0=ALU.add,
                        op1=ALU.mult,
                    )

        def affine(g):
            planes = pl.tile([P, PACK, GROUP], BF16, tag="planes", name="planes%d" % g)
            for j in range(PACK):
                nc.scalar.activation(
                    out=planes[:, j, :],
                    in_=st[("banks", g)][j][:],
                    func=ACT.Identity,
                    scale=ln_col[:, j : j + 1],
                    bias=ln_col[:, PACK + j : PACK + j + 1],
                )
            st[("planes", g)] = planes

        def regroup(g):
            grouped = gr.tile([P, GROUP, PACK], BF16, tag="grouped", name="grouped%d" % g, align_bytes=64)
            dst = grouped[:].rearrange("p (c i) t -> p c t i", i=8)
            src = st[("planes", g)][:].rearrange("p t (c i) -> p c t i", i=8)
            if t4_on_vector(g):
                nc.vector.tensor_copy(out=dst, in_=src)
            else:
                nc.scalar.copy(out=dst, in_=src)
            st[("grouped", g)] = grouped

        def quantise(g):
            codes = cd.tile([P, GROUP], U32, tag="codes", name="codes%d" % g, align_bytes=64)
            scl = cd.tile([P, GROUP], U8, tag="scl", name="scl%d" % g, align_bytes=64)
            nc.vector.quantize_mx(
                out=codes[:].bitcast(FP8X4),
                scales=scl[:],
                in_=st[("grouped", g)][:].rearrange("p c t -> p (c t)"),
            )
            st[("codes", g)] = codes
            st[("scl", g)] = scl

        def project(g):
            obs = []
            for n in range(NT):
                ob = psum.tile([P, OUTS], FP32, tag="o", name="ob%d_%d" % (g, n))
                nc.tensor.matmul_mx(
                    out=ob[:],
                    lhsT=st[("codes", g)][:, n * P : (n + 1) * P].bitcast(FP8X4),
                    lhsT_scale=st[("scl", g)][:, n * P : (n + 1) * P],
                    rhs=w_codes[:].bitcast(FP8X4),
                    rhs_scale=w_scales[:],
                    start=True,
                    stop=True,
                )
                obs.append(ob)
            st[("obs", g)] = obs

        def finish(g):
            res = rs.tile([P, 2, NT, HALF], FP32, tag="res", name="res%d" % g)
            bias_v = bias_sb[:].rearrange("p (h o) -> p h o", h=2)
            for n in range(NT):
                ob_v = st[("obs", g)][n][:].rearrange("p (h o) -> p h o", h=2)
                if sg_bank(g, n):
                    nc.scalar.copy(out=res[:, :, n, :], in_=ob_v)
                    nc.gpsimd.tensor_tensor(out=res[:, :, n, :], in0=res[:, :, n, :], in1=bias_v, op=ALU.add)
                else:
                    nc.vector.tensor_tensor(out=res[:, :, n, :], in0=ob_v, in1=bias_v, op=ALU.add)
            rows = slice(g * GROUP, (g + 1) * GROUP)
            nc.sync.dma_start(out=kf[rows, :].rearrange("(p n) o -> p n o", n=NT), in_=res[:, 0, :, :])
            nc.sync.dma_start(out=vf[rows, :].rearrange("(p n) o -> p n o", n=NT), in_=res[:, 1, :, :])

        def regroup_by_tile(g):
            grouped = gr.tile([P, GROUP, PACK], BF16, tag="grouped", name="grouped%d" % g, align_bytes=64)
            for n in range(NT):
                cols = slice(n * P, (n + 1) * P)
                nc.scalar.copy(
                    out=grouped[:, cols, :].rearrange("p (c i) t -> p c t i", i=8),
                    in_=st[("planes", g)][:, :, cols].rearrange("p t (c i) -> p c t i", i=8),
                )
            st[("grouped", g)] = grouped

        def end_by_tile(g):
            codes = cd.tile([P, GROUP], U32, tag="codes", name="codes%d" % g, align_bytes=64)
            scl = cd.tile([P, GROUP], U8, tag="scl", name="scl%d" % g, align_bytes=64)
            res = rs.tile([P, 2, NT, HALF], FP32, tag="res", name="res%d" % g)
            bias_v = bias_sb[:].rearrange("p (h o) -> p h o", h=2)
            rows = slice(g * GROUP, (g + 1) * GROUP)
            obs = []

            def front(n):
                cols = slice(n * P, (n + 1) * P)
                nc.vector.quantize_mx(
                    out=codes[:, cols].bitcast(FP8X4),
                    scales=scl[:, cols],
                    in_=st[("grouped", g)][:, cols, :].rearrange("p c t -> p (c t)"),
                )
                ob = psum.tile([P, OUTS], FP32, tag="o", name="ob%d_%d" % (g, n))
                nc.tensor.matmul_mx(
                    out=ob[:],
                    lhsT=codes[:, cols].bitcast(FP8X4),
                    lhsT_scale=scl[:, cols],
                    rhs=w_codes[:].bitcast(FP8X4),
                    rhs_scale=w_scales[:],
                    start=True,
                    stop=True,
                )
                obs.append(ob)

            def back(n):
                nc.vector.tensor_tensor(
                    out=res[:, :, n, :], in0=obs[n][:].rearrange("p (h o) -> p h o", h=2), in1=bias_v, op=ALU.add
                )
                nc.sync.dma_start(out=kf[rows, :].rearrange("(p n) o -> p n o", n=NT)[:, n, :], in_=res[:, 0, n, :])
                nc.sync.dma_start(out=vf[rows, :].rearrange("(p n) o -> p n o", n=NT)[:, n, :], in_=res[:, 1, n, :])

            front(0)
            for n in range(1, NT):
                front(n)
                back(n - 1)
            back(NT - 1)

        def stats(g):
            stats_open(g)
            for n in range(NT):
                stats_tile(g, n)
            stats_close(g)

        def scalars_and_normalise(g):
            recip(g)
            neg_mean(g)
            normalise(g)

        def live(g):
            return 0 <= g < NG

        x_first = xin.tile([P, NT, FEATS], BF16, tag="x", name="x_sb0")
        st[("x", 0)] = x_first
        for n in range(NT):
            nc.sync.dma_start(
                out=x_first[:, n, :], in_=xf[0:GROUP, :].rearrange("(p n) f -> p n f", n=NT)[:, n, :]
            )
        w_raw = const.tile([P, 4, FEATS], BF16)
        nc.sync.dma_start(out=w_raw[:, 0:2, :], in_=Wk.rearrange("(c p) f -> p c f", p=P))
        nc.sync.dma_start(out=w_raw[:, 2:4, :], in_=Wv.rearrange("(c p) f -> p c f", p=P))
        ln_w_raw = const.tile([P, PACK], BF16)
        ln_b_raw = const.tile([P, PACK], BF16)
        nc.scalar.dma_start(out=ln_w_raw[:], in_=ln_k_w.rearrange("(p t) -> p t", t=PACK))
        nc.scalar.dma_start(out=ln_b_raw[:], in_=ln_k_b.rearrange("(p t) -> p t", t=PACK))
        for g in range(1, NG):
            load(g)
        ident_f = const.tile([P, P], FP32)
        make_identity(nc, ident_f[:])

        first_group()

        ln_col = const.tile([P, 8], FP32)
        nc.scalar.copy(out=ln_col[:, 0:PACK], in_=ln_w_raw[:])
        nc.scalar.copy(out=ln_col[:, PACK : 2 * PACK], in_=ln_b_raw[:])

        w_grp = const.tile([P, OUTS, PACK], BF16, align_bytes=64)
        w_words = w_raw[:].bitcast(FP32)
        for h in range(2):
            wt = psum.tile([P, 2, HALF], FP32, tag="o", name="wt%d" % h)
            for u in range(2):
                for c in range(2):
                    nc.tensor.transpose(
                        wt[:, u, c * P : (c + 1) * P], w_words[:, 2 * h + c, u : FEATS // 2 : 2], ident_f[:]
                    )
            nc.scalar.copy(
                out=w_grp[:, h * HALF : (h + 1) * HALF, :].bitcast(FP32), in_=wt[:].rearrange("p u o -> p o u")
            )
        w_codes = const.tile([P, OUTS], U32, align_bytes=64)
        w_scales = const.tile([P, OUTS], U8, align_bytes=64)
        bias_sb = const.tile([P, OUTS], BF16)

        transposes(0)
        for n in range(1, vector_tiles(1)):
            stats_tile(1, n)
        stats_close(1)
        scalar_stats(1)
        root(1)
        stats_open(2)
        stats_tile(2, 0)
        scalars_and_normalise(1)
        nc.scalar.dma_start(out=bias_sb[:, 0:HALF], in_=bk.partition_broadcast(P))
        nc.scalar.dma_start(out=bias_sb[:, HALF:OUTS], in_=bv.partition_broadcast(P))
        for n in range(1, NT):
            stats_tile(2, n)
        stats_close(2)

        for i in range(NG + 1):
            late = SOON < i < NG
            if i == NG - 1:
                end_by_tile(i - 1)
            elif late:
                quantise(i - 1)
                project(i - 1)
            if live(i + 2) and i >= 2:
                root(i + 2)
            if live(i):
                affine(i)
            if live(i + 1):
                transposes(i + 1)
            if live(i + 2) and i < 2:
                root(i + 2)
            if i >= NG - 2 and live(i):
                regroup_by_tile(i)
            elif live(i):
                regroup(i)
            if live(i + 3):
                stats(i + 3)
            if live(i + 2):
                scalars_and_normalise(i + 2)
            if i == 0:
                nc.vector.quantize_mx(
                    out=w_codes[:].bitcast(FP8X4), scales=w_scales[:], in_=w_grp[:].rearrange("p o j -> p (o j)")
                )
            if late and i < NG - 1:
                finish(i - 1)
            elif i == NG:
                end_by_tile(NG - 1)
            elif i <= SOON:
                if live(i - 1):
                    quantise(i - 1)
                if live(i - 2):
                    finish(i - 2)
                if live(i - 1):
                    project(i - 1)
                if i == SOON:
                    finish(i - 1)
